import numpy as np
import ml_dtypes


def mxq(x, axis, fmt="e4m3"):
    dtype, down = {"e4m3": (ml_dtypes.float8_e4m3fn, 7), "e5m2": (ml_dtypes.float8_e5m2, 14)}[fmt]
    v = np.moveaxis(np.asarray(x, np.float32).astype(ml_dtypes.bfloat16).astype(np.float64), axis, -1)
    blocks = v.reshape(v.shape[:-1] + (-1, 32))
    amax = np.abs(blocks).max(-1, keepdims=True)
    byte = np.maximum(np.where(amax > 0, np.frexp(amax)[1] - 1 + 127, 0) - down, 1)
    scale = np.exp2(byte - 127.0)
    codes = (blocks / scale).astype(np.float32).astype(dtype).astype(np.float64)
    return np.moveaxis((codes * scale).reshape(v.shape), -1, axis)


WIDE = False


def mx_kscale(k):
    if not WIDE:
        return np.ones(k)
    levels = np.array([10, -10, 5, -5, 0])
    a = np.random.permutation(np.resize(levels, k // 512 * 4)).reshape(k // 512, 4)
    idx = np.arange(k)
    return np.exp2(a[idx // 512, idx % 128 // 32])


BF16 = ml_dtypes.bfloat16


def bf(x):
    return np.asarray(x, np.float32).astype(BF16)


def f64(x):
    return np.asarray(x).astype(np.float64)


B, Nb1, Nw1, Nb2x, Nb2y, Nw2x, Nw2y, R, C = 4096, 2, 16, 1, 1, 32, 16, 128, 2
J1 = Nb1 * Nb1
J3 = Nb2x * Nb2y
J2 = J3 * J1
K3 = J1 * R
L3 = C * Nw2x * Nw2y


def setup_inputs():
    t = mx_kscale(K3)
    tt = np.tile(t.reshape(J1, R), (J3, 1))
    return {"h_switch": bf(np.random.standard_normal((B, J2, R))),
            "k2": bf(np.random.standard_normal((J2, R, R)) / np.sqrt(R) * tt[:, None, :]),
            "b2": bf(np.random.standard_normal((1, J2, R)) * 0.3 * tt[None]),
            "k3": bf(np.random.standard_normal((J3, K3, L3)) / np.sqrt(K3) / t[None, :, None]),
            "b3": bf(np.random.standard_normal((1, J3, L3)) * 0.3)}


def reference(h_switch, k2, b2, k3, b3):
    g = (f64(h_switch).transpose(1, 0, 2) @ f64(k2)).transpose(1, 0, 2) + f64(b2)
    g = g.reshape(B, J3, K3)
    gq = mxq(g, 2, "e4m3").transpose(1, 0, 2)
    y = (gq @ mxq(f64(k3), 1, "e4m3")).transpose(1, 0, 2) + f64(b3)
    y = y.reshape(B, Nb2x, Nb2y, Nw2x, Nw2y, C).transpose(0, 1, 3, 2, 4, 5)
    return y.reshape(B, Nb2x * Nw2x, Nb2y * Nw2y, C)

@@ -1,0 +1,213 @@
+from contextlib import ExitStack
+
+import concourse.masks as masks
+import concourse.mybir as mybir
+
+BF16 = mybir.dt.bfloat16
+F32 = mybir.dt.float32
+U32 = mybir.dt.uint32
+U8 = mybir.dt.uint8
+FP8X4 = mybir.dt.float8_e4m3fn_x4
+ADD = mybir.AluOpType.add
+
+P = 128
+GROUPS = 4
+SAMPLES = 4096
+TILES = SAMPLES // P
+RT = 2
+ROUNDS = TILES // RT
+L = 1024
+HALF = 512
+H_CHUNKS = [2, 2, 4, 8, 8, 8]
+
+FLOPS = 2 * SAMPLES * GROUPS * P * P + 2 * SAMPLES * GROUPS * P * L
+
+
+def tile_switchnet_fstar_pb_t_kernel(tc, h_switch, k2, b2, k3, b3, out):
+    nc = tc.nc
+    h_view = h_switch.rearrange("(p t) j r -> p t (j r)", t=TILES)
+    out_view = out.rearrange("(p t) x y c -> p t (x y c)", t=TILES)
+    k3_view = k3.rearrange("o (t p) n -> p (o t) n", p=P)
+
+    with ExitStack() as ctx:
+        ctx.enter_context(tc.manual_schedule())
+        const = ctx.enter_context(tc.tile_pool(name="const", bufs=1))
+        ht_pool = ctx.enter_context(tc.tile_pool(name="ht", bufs=3))
+        grp_pool = ctx.enter_context(tc.tile_pool(name="grp", bufs=3))
+        q_pool = ctx.enter_context(tc.tile_pool(name="q", bufs=3))
+        y_pool = ctx.enter_context(tc.tile_pool(name="ysb", bufs=4))
+        ps_t = ctx.enter_context(tc.psum_pool(name="pst", bufs=2))
+        ps_g = ctx.enter_context(tc.psum_pool(name="psg", bufs=2))
+        ps_y = ctx.enter_context(tc.psum_pool(name="psy", bufs=4))
+
+        b2z = const.tile([P, P], BF16, name="b2z")
+        b3z = const.tile([P, L], BF16, name="b3z")
+        ones = const.tile([P, P], BF16, name="ones")
+        ident = const.tile([P, P], BF16, name="ident")
+        nc.vector.memset(b2z[:], 0.0)
+        nc.vector.memset(b3z[:], 0.0)
+        nc.vector.memset(ones[:], 1.0)
+        masks.make_identity(nc, ident[:])
+        nc.scalar.dma_start(out=b2z[0:GROUPS, :], in_=b2.rearrange("o j r -> (o j) r"))
+        nc.scalar.dma_start(out=b3z[0:1, :], in_=b3.rearrange("o j l -> (o j) l"))
+
+        h_of = []
+        h_tiles = []
+        t0 = 0
+        for c, n in enumerate(H_CHUNKS):
+            hc = const.tile([P, n, GROUPS * P], BF16, name="h%d" % c)
+            h_tiles.append((hc, t0, n))
+            for i in range(n):
+                h_of.append((hc, i))
+            t0 += n
+        k2_sb = const.tile([P, GROUPS, P], BF16, name="k2sb")
+        k3r = [const.tile([P, GROUPS, HALF], BF16, name="k3r%d" % i) for i in range(2)]
+        k3g = [const.tile([P, HALF, GROUPS], BF16, name="k3g%d" % i, align_bytes=64) for i in range(2)]
+        k3c = const.tile([P, L], U32, name="k3c", align_bytes=64)
+        k3s = const.tile([P, L], U8, name="k3s", align_bytes=64)
+
+        def load_h(c):
+            hc, start, n = h_tiles[c]
+            nc.sync.dma_start(out=hc[:], in_=h_view[:, start:start + n, :])
+
+        load_h(0)
+        nc.sync.dma_start(out=k2_sb[:], in_=k2.rearrange("j k m -> k j m"))
+        for i in range(2):
+            nc.sync.dma_start(out=k3r[i][:], in_=k3_view[:, :, i * HALF:(i + 1) * HALF])
+        for c in range(1, len(H_CHUNKS)):
+            load_h(c)
+
+        b2f = const.tile([P, GROUPS], F32, name="b2f")
+        b3f = const.tile([P, L], F32, name="b3f")
+
+        def spread_biases():
+            tpb = ps_t.tile([P, RT, GROUPS, P], BF16, name="tp", tag="tp")
+            nc.tensor.transpose(tpb[:, 0, 0, :], b2z[:], ident[:])
+            nc.vector.tensor_copy(out=b2f[:], in_=tpb[:, 0, 0, 0:GROUPS])
+            for i in range(2):
+                yb = ps_y.tile([P, HALF], F32, name="y", tag="y")
+                nc.tensor.matmul(yb[:], lhsT=ones[:], rhs=b3z[:, i * HALF:(i + 1) * HALF], start=True, stop=True)
+                nc.scalar.copy(out=b3f[:, i * HALF:(i + 1) * HALF], in_=yb[:])
+
+        def regroup_k3(engine_copy, i, n0, n1):
+            engine_copy(
+                out=k3g[i][:, n0:n1, :].rearrange("p (c i) t -> p c t i", i=4),
+                in_=k3r[i][:, :, n0:n1].rearrange("p t (c i) -> p c t i", i=4),
+            )
+
+        def quantise_k3(i):
+            nc.vector.quantize_mx(
+                out=k3c[:, i * HALF:(i + 1) * HALF].bitcast(FP8X4),
+                scales=k3s[:, i * HALF:(i + 1) * HALF],
+                in_=k3g[i][:].rearrange("p n t -> p (n t)"),
+            )
+
+        def transposes(r):
+            tp = ps_t.tile([P, RT, GROUPS, P], BF16, name="tp", tag="tp")
+            for a in range(RT):
+                hc, off = h_of[RT * r + a]
+                for j in range(GROUPS):
+                    nc.tensor.transpose(tp[:, a, j, :], hc[:, off, j * P:(j + 1) * P], ident[:])
+            ht = ht_pool.tile([P, RT, GROUPS, P], BF16, name="ht", tag="ht")
+            nc.scalar.copy(out=ht[:], in_=tp[:])
+            return ht
+
+        def stage1(ht):
+            grp = grp_pool.tile([P, RT, P, GROUPS], BF16, name="grp", tag="grp", align_bytes=64)
+            for a in range(RT):
+                g = ps_g.tile([P, GROUPS, P], F32, name="g", tag="g")
+                for j in range(GROUPS):
+                    nc.tensor.matmul(g[:, j, :], lhsT=k2_sb[:, j, :], rhs=ht[:, a, j, :], start=True, stop=True)
+                nc.vector.tensor_tensor(
+                    out=grp[:, a],
+                    in0=g[:].rearrange("p j b -> p b j"),
+                    in1=b2f[:].unsqueeze(1).to_broadcast([P, P, GROUPS]),
+                    op=ADD,
+                )
+            return grp
+
+        def quantise(grp):
+            codes = q_pool.tile([P, RT * P], U32, name="codes", tag="codes", align_bytes=64)
+            scl = q_pool.tile([P, RT * P], U8, name="scl", tag="scl", align_bytes=64)
+            nc.vector.quantize_mx(
+                out=codes[:].bitcast(FP8X4),
+                scales=scl[:],
+                in_=grp[:].rearrange("p a b j -> p (a b j)"),
+            )
+            return codes, scl
+
+        ysbs = {}
+
+        def stage2(r, codes, scl):
+            q = r // 2
+            if r % 2 == 0:
+                ysbs[q] = y_pool.tile([P, 2 * RT, L], F32, name="ysb", tag="ysb")
+            ysb = ysbs[q]
+            for a in range(RT):
+                row = RT * (r % 2) + a
+                for i in range(2):
+                    y = ps_y.tile([P, HALF], F32, name="y", tag="y")
+                    nc.tensor.matmul_mx(
+                        out=y[:],
+                        lhsT=codes[:, a * P:(a + 1) * P].bitcast(FP8X4),
+                        lhsT_scale=scl[:, a * P:(a + 1) * P],
+                        rhs=k3c[:, i * HALF:(i + 1) * HALF].bitcast(FP8X4),
+                        rhs_scale=k3s[:, i * HALF:(i + 1) * HALF],
+                        start=True,
+                        stop=True,
+                    )
+                    if i == 0 or r == ROUNDS - 1:
+                        nc.vector.tensor_tensor(
+                            out=ysb[:, row, i * HALF:(i + 1) * HALF], in0=y[:],
+                            in1=b3f[:, i * HALF:(i + 1) * HALF], op=ADD)
+                    else:
+                        nc.scalar.copy(out=ysb[:, row, HALF:L], in_=y[:])
+                if r == ROUNDS - 1:
+                    t = RT * r + a
+                    nc.sync.dma_start(out=out_view[:, t:t + 1, :], in_=ysb[:, row:row + 1, :])
+
+        def add_b3(ysb, row0, rows):
+            nc.gpsimd.tensor_tensor(
+                out=ysb[:, row0:row0 + rows, HALF:L],
+                in0=ysb[:, row0:row0 + rows, HALF:L],
+                in1=b3f[:, HALF:L].unsqueeze(1).to_broadcast([P, rows, HALF]),
+                op=ADD,
+            )
+
+        def finish(r):
+            q = r // 2
+            ysb = ysbs[q]
+            if r == ROUNDS - 2:
+                add_b3(ysb, 0, RT)
+                nc.sync.dma_start(out=out_view[:, RT * r:RT * (r + 1), :], in_=ysb[:, 0:RT, :])
+            elif r % 2 == 1 and r < ROUNDS - 2:
+                add_b3(ysb, 0, 2 * RT)
+                nc.sync.dma_start(out=out_view[:, RT * (r - 1):RT * (r + 1), :], in_=ysb[:])
+
+        hts = {}
+        grps = {}
+        qs = {}
+        hts[0] = transposes(0)
+        spread_biases()
+        regroup_k3(nc.vector.tensor_copy, 0, 0, HALF)
+        regroup_k3(nc.vector.tensor_copy, 1, 0, HALF // 2)
+        regroup_k3(nc.scalar.copy, 1, HALF // 2, HALF)
+        grps[0] = stage1(hts[0])
+        hts[1] = transposes(1)
+        quantise_k3(0)
+        qs[0] = quantise(grps[0])
+        quantise_k3(1)
+        grps[1] = stage1(hts[1])
+        hts[2] = transposes(2)
+        stage2(0, qs[0][0], qs[0][1])
+        qs[1] = quantise(grps[1])
+        finish(0)
+        for s in range(3, ROUNDS + 2):
+            if s < ROUNDS:
+                hts[s] = transposes(s)
+            if s <= ROUNDS:
+                grps[s - 1] = stage1(hts[s - 1])
+            stage2(s - 2, qs[s - 2][0], qs[s - 2][1])
+            if s <= ROUNDS:
+                qs[s - 1] = quantise(grps[s - 1])
+            finish(s - 2)

@@ -9,12 +9,15 @@ U32 = mybir.dt.uint32
 U8 = mybir.dt.uint8
 FP8X4 = mybir.dt.float8_e4m3fn_x4
 ADD = mybir.AluOpType.add
+MULT = mybir.AluOpType.mult
+IDENT = mybir.ActivationFunctionType.Identity
 
 P = 128
 GROUPS = 4
 SAMPLES = 4096
 TILES = SAMPLES // P
 RT = 2
+RB = RT * P
 ROUNDS = TILES // RT
 L = 1024
 HALF = 512
@@ -32,10 +35,11 @@ def tile_switchnet_fstar_pb_t_kernel(tc, h_switch, k2, b2, k3, b3, out):
     with ExitStack() as ctx:
         ctx.enter_context(tc.manual_schedule())
         const = ctx.enter_context(tc.tile_pool(name="const", bufs=1))
-        ht_pool = ctx.enter_context(tc.tile_pool(name="ht", bufs=3))
-        grp_pool = ctx.enter_context(tc.tile_pool(name="grp", bufs=3))
+        ht_pool = ctx.enter_context(tc.tile_pool(name="ht", bufs=4))
+        gs_pool = ctx.enter_context(tc.tile_pool(name="gs", bufs=3))
+        grp_pool = ctx.enter_context(tc.tile_pool(name="grp", bufs=1))
         q_pool = ctx.enter_context(tc.tile_pool(name="q", bufs=3))
-        y_pool = ctx.enter_context(tc.tile_pool(name="ysb", bufs=4))
+        y_pool = ctx.enter_context(tc.tile_pool(name="ysb", bufs=5))
         ps_t = ctx.enter_context(tc.psum_pool(name="pst", bufs=2))
         ps_g = ctx.enter_context(tc.psum_pool(name="psg", bufs=2))
         ps_y = ctx.enter_context(tc.psum_pool(name="psy", bufs=4))
@@ -72,16 +76,17 @@ def tile_switchnet_fstar_pb_t_kernel(tc, h_switch, k2, b2, k3, b3, out):
 
         load_h(0)
         nc.sync.dma_start(out=k2_sb[:], in_=k2.rearrange("j k m -> k j m"))
+        load_h(1)
         for i in range(2):
             nc.sync.dma_start(out=k3r[i][:], in_=k3_view[:, :, i * HALF:(i + 1) * HALF])
-        for c in range(1, len(H_CHUNKS)):
+        for c in range(2, len(H_CHUNKS)):
             load_h(c)
 
         b2f = const.tile([P, GROUPS], F32, name="b2f")
         b3f = const.tile([P, L], F32, name="b3f")
 
         def spread_biases():
-            tpb = ps_t.tile([P, RT, GROUPS, P], BF16, name="tp", tag="tp")
+            tpb = ps_t.tile([P, GROUPS, RT, P], BF16, name="tp", tag="tp")
             nc.tensor.transpose(tpb[:, 0, 0, :], b2z[:], ident[:])
             nc.vector.tensor_copy(out=b2f[:], in_=tpb[:, 0, 0, 0:GROUPS])
             for i in range(2):
@@ -102,112 +107,143 @@ def tile_switchnet_fstar_pb_t_kernel(tc, h_switch, k2, b2, k3, b3, out):
                 in_=k3g[i][:].rearrange("p n t -> p (n t)"),
             )
 
+        hts = {}
+        gps = {}
+        gss = {}
+        grps = {}
+        qs = {}
+        yps = {}
+        ysbs = {}
+
         def transposes(r):
-            tp = ps_t.tile([P, RT, GROUPS, P], BF16, name="tp", tag="tp")
+            tp = ps_t.tile([P, GROUPS, RT, P], BF16, name="tp", tag="tp")
             for a in range(RT):
                 hc, off = h_of[RT * r + a]
                 for j in range(GROUPS):
-                    nc.tensor.transpose(tp[:, a, j, :], hc[:, off, j * P:(j + 1) * P], ident[:])
-            ht = ht_pool.tile([P, RT, GROUPS, P], BF16, name="ht", tag="ht")
+                    nc.tensor.transpose(tp[:, j, a, :], hc[:, off, j * P:(j + 1) * P], ident[:])
+            ht = ht_pool.tile([P, GROUPS, RT, P], BF16, name="ht", tag="ht")
             nc.scalar.copy(out=ht[:], in_=tp[:])
-            return ht
+            hts[r] = ht
 
-        def stage1(ht):
-            grp = grp_pool.tile([P, RT, P, GROUPS], BF16, name="grp", tag="grp", align_bytes=64)
+        def new_grp(r):
+            grps[r] = grp_pool.tile([P, RB, GROUPS], BF16, name="grp", tag="grp", align_bytes=64)
+
+        def stage1_on_vector(r):
+            new_grp(r)
             for a in range(RT):
                 g = ps_g.tile([P, GROUPS, P], F32, name="g", tag="g")
                 for j in range(GROUPS):
-                    nc.tensor.matmul(g[:, j, :], lhsT=k2_sb[:, j, :], rhs=ht[:, a, j, :], start=True, stop=True)
+                    nc.tensor.matmul(g[:, j, :], lhsT=k2_sb[:, j, :], rhs=hts[r][:, j, a, :], start=True, stop=True)
                 nc.vector.tensor_tensor(
-                    out=grp[:, a],
+                    out=grps[r][:, a * P:(a + 1) * P, :],
                     in0=g[:].rearrange("p j b -> p b j"),
                     in1=b2f[:].unsqueeze(1).to_broadcast([P, P, GROUPS]),
                     op=ADD,
                 )
-            return grp
 
-        def quantise(grp):
-            codes = q_pool.tile([P, RT * P], U32, name="codes", tag="codes", align_bytes=64)
-            scl = q_pool.tile([P, RT * P], U8, name="scl", tag="scl", align_bytes=64)
+        def stage1(r):
+            gps[r] = []
+            for hb in range(2):
+                g = ps_g.tile([P, 2, RB], F32, name="g", tag="g")
+                for jj in range(2):
+                    j = 2 * hb + jj
+                    nc.tensor.matmul(
+                        g[:, jj, :], lhsT=k2_sb[:, j, :],
+                        rhs=hts[r][:, j, :, :].rearrange("p a b -> p (a b)"), start=True, stop=True)
+                gps[r].append(g)
+            gss[r] = gs_pool.tile([P, GROUPS, RB], BF16, name="gs", tag="gs")
+
+        def add_b2(r, hb):
+            for jj in range(2):
+                j = 2 * hb + jj
+                nc.scalar.activation(
+                    out=gss[r][:, j, :], in_=gps[r][hb][:, jj, :], func=IDENT,
+                    bias=b2f[:, j:j + 1], scale=1.0)
+
+        def regroup(r):
+            new_grp(r)
+            nc.gpsimd.tensor_scalar(
+                out=grps[r][:], in0=gss[r][:].rearrange("p j b -> p b j"),
+                scalar1=1.0, scalar2=0.0, op0=MULT, op1=ADD)
+
+        def quantise(r):
+            codes = q_pool.tile([P, RB], U32, name="codes", tag="codes", align_bytes=64)
+            scl = q_pool.tile([P, RB], U8, name="scl", tag="scl", align_bytes=64)
             nc.vector.quantize_mx(
                 out=codes[:].bitcast(FP8X4),
                 scales=scl[:],
-                in_=grp[:].rearrange("p a b j -> p (a b j)"),
+                in_=grps[r][:].rearrange("p b j -> p (b j)"),
             )
-            return codes, scl
+            qs[r] = (codes, scl)
 
-        ysbs = {}
-
-        def stage2(r, codes, scl):
-            q = r // 2
-            if r % 2 == 0:
-                ysbs[q] = y_pool.tile([P, 2 * RT, L], F32, name="ysb", tag="ysb")
-            ysb = ysbs[q]
-            for a in range(RT):
-                row = RT * (r % 2) + a
-                for i in range(2):
-                    y = ps_y.tile([P, HALF], F32, name="y", tag="y")
-                    nc.tensor.matmul_mx(
-                        out=y[:],
-                        lhsT=codes[:, a * P:(a + 1) * P].bitcast(FP8X4),
-                        lhsT_scale=scl[:, a * P:(a + 1) * P],
-                        rhs=k3c[:, i * HALF:(i + 1) * HALF].bitcast(FP8X4),
-                        rhs_scale=k3s[:, i * HALF:(i + 1) * HALF],
-                        start=True,
-                        stop=True,
-                    )
-                    if i == 0 or r == ROUNDS - 1:
-                        nc.vector.tensor_tensor(
-                            out=ysb[:, row, i * HALF:(i + 1) * HALF], in0=y[:],
-                            in1=b3f[:, i * HALF:(i + 1) * HALF], op=ADD)
-                    else:
-                        nc.scalar.copy(out=ysb[:, row, HALF:L], in_=y[:])
-                if r == ROUNDS - 1:
-                    t = RT * r + a
-                    nc.sync.dma_start(out=out_view[:, t:t + 1, :], in_=ysb[:, row:row + 1, :])
-
-        def add_b3(ysb, row0, rows):
-            nc.gpsimd.tensor_tensor(
-                out=ysb[:, row0:row0 + rows, HALF:L],
-                in0=ysb[:, row0:row0 + rows, HALF:L],
-                in1=b3f[:, HALF:L].unsqueeze(1).to_broadcast([P, rows, HALF]),
-                op=ADD,
+        def mx_pass(r, k):
+            a, i = k // 2, k % 2
+            codes, scl = qs[r]
+            y = ps_y.tile([P, HALF], F32, name="y", tag="y")
+            nc.tensor.matmul_mx(
+                out=y[:],
+                lhsT=codes[:, a * P:(a + 1) * P].bitcast(FP8X4),
+                lhsT_scale=scl[:, a * P:(a + 1) * P],
+                rhs=k3c[:, i * HALF:(i + 1) * HALF].bitcast(FP8X4),
+                rhs_scale=k3s[:, i * HALF:(i + 1) * HALF],
+                start=True,
+                stop=True,
             )
+            yps[(r, k)] = y
 
-        def finish(r):
-            q = r // 2
-            ysb = ysbs[q]
-            if r == ROUNDS - 2:
-                add_b3(ysb, 0, RT)
-                nc.sync.dma_start(out=out_view[:, RT * r:RT * (r + 1), :], in_=ysb[:, 0:RT, :])
-            elif r % 2 == 1 and r < ROUNDS - 2:
-                add_b3(ysb, 0, 2 * RT)
-                nc.sync.dma_start(out=out_view[:, RT * (r - 1):RT * (r + 1), :], in_=ysb[:])
+        def empty_y(r, k):
+            a, i = k // 2, k % 2
+            if k == 0:
+                ysbs[r] = y_pool.tile([P, RT, L], F32, name="ysb", tag="ysb")
+            nc.vector.tensor_tensor(
+                out=ysbs[r][:, a, i * HALF:(i + 1) * HALF], in0=yps[(r, k)][:],
+                in1=b3f[:, i * HALF:(i + 1) * HALF], op=ADD)
+            if r == ROUNDS - 1 and i == 1:
+                t = RT * r + a
+                nc.sync.dma_start(out=out_view[:, t:t + 1, :], in_=ysbs[r][:, a:a + 1, :])
+            if r < ROUNDS - 1 and k == 3:
+                nc.sync.dma_start(out=out_view[:, RT * r:RT * (r + 1), :], in_=ysbs[r][:])
 
-        hts = {}
-        grps = {}
-        qs = {}
-        hts[0] = transposes(0)
+        transposes(0)
         spread_biases()
         regroup_k3(nc.vector.tensor_copy, 0, 0, HALF)
-        regroup_k3(nc.vector.tensor_copy, 1, 0, HALF // 2)
+        stage1_on_vector(0)
+        transposes(1)
         regroup_k3(nc.scalar.copy, 1, HALF // 2, HALF)
-        grps[0] = stage1(hts[0])
-        hts[1] = transposes(1)
+        regroup_k3(nc.vector.tensor_copy, 1, 0, HALF // 2)
+        stage1(1)
+        add_b2(1, 0)
+        transposes(2)
+        add_b2(1, 1)
+        transposes(3)
         quantise_k3(0)
-        qs[0] = quantise(grps[0])
         quantise_k3(1)
-        grps[1] = stage1(hts[1])
-        hts[2] = transposes(2)
-        stage2(0, qs[0][0], qs[0][1])
-        qs[1] = quantise(grps[1])
-        finish(0)
-        for s in range(3, ROUNDS + 2):
-            if s < ROUNDS:
-                hts[s] = transposes(s)
-            if s <= ROUNDS:
-                grps[s - 1] = stage1(hts[s - 1])
-            stage2(s - 2, qs[s - 2][0], qs[s - 2][1])
-            if s <= ROUNDS:
-                qs[s - 1] = quantise(grps[s - 1])
-            finish(s - 2)
+        quantise(0)
+        regroup(1)
+        stage1(2)
+        add_b2(2, 0)
+        add_b2(2, 1)
+        for k in range(4):
+            mx_pass(0, k)
+        for s in range(ROUNDS):
+            if s + 4 < ROUNDS:
+                transposes(s + 4)
+            if s + 3 < ROUNDS:
+                stage1(s + 3)
+                add_b2(s + 3, 0)
+                add_b2(s + 3, 1)
+            empty_y(s, 0)
+            empty_y(s, 1)
+            if s + 1 < ROUNDS:
+                quantise(s + 1)
+            if s + 2 < ROUNDS:
+                regroup(s + 2)
+            if s + 1 < ROUNDS:
+                mx_pass(s + 1, 0)
+                mx_pass(s + 1, 1)
+            empty_y(s, 2)
+            if s + 1 < ROUNDS:
+                mx_pass(s + 1, 2)
+            empty_y(s, 3)
+            if s + 1 < ROUNDS:
+                mx_pass(s + 1, 3)

@@ -52,8 +52,10 @@ def tile_switchnet_fstar_pb_t_kernel(tc, h_switch, k2, b2, k3, b3, out):
         nc.vector.memset(b3z[:], 0.0)
         nc.vector.memset(ones[:], 1.0)
         masks.make_identity(nc, ident[:])
-        nc.scalar.dma_start(out=b2z[0:GROUPS, :], in_=b2.rearrange("o j r -> (o j) r"))
-        nc.scalar.dma_start(out=b3z[0:1, :], in_=b3.rearrange("o j l -> (o j) l"))
+
+        warm = const.tile([P, 2], F32, name="warm")
+        nc.vector.memset(warm[:], 0.0)
+        nc.scalar.activation(out=warm[:, 1:2], in_=warm[:, 0:1], func=IDENT, bias=0.0, scale=1.0)
 
         h_of = []
         h_tiles = []
@@ -76,6 +78,8 @@ def tile_switchnet_fstar_pb_t_kernel(tc, h_switch, k2, b2, k3, b3, out):
 
         load_h(0)
         nc.sync.dma_start(out=k2_sb[:], in_=k2.rearrange("j k m -> k j m"))
+        nc.sync.dma_start(out=b2z[0:GROUPS, :], in_=b2.rearrange("o j r -> (o j) r"))
+        nc.sync.dma_start(out=b3z[0:1, :], in_=b3.rearrange("o j l -> (o j) l"))
         load_h(1)
         for i in range(2):
             nc.sync.dma_start(out=k3r[i][:], in_=k3_view[:, :, i * HALF:(i + 1) * HALF])
@@ -107,6 +111,7 @@ def tile_switchnet_fstar_pb_t_kernel(tc, h_switch, k2, b2, k3, b3, out):
                 in_=k3g[i][:].rearrange("p n t -> p (n t)"),
             )
 
+        tps = {}
         hts = {}
         gps = {}
         gss = {}
@@ -121,8 +126,11 @@ def tile_switchnet_fstar_pb_t_kernel(tc, h_switch, k2, b2, k3, b3, out):
                 hc, off = h_of[RT * r + a]
                 for j in range(GROUPS):
                     nc.tensor.transpose(tp[:, j, a, :], hc[:, off, j * P:(j + 1) * P], ident[:])
+            tps[r] = tp
+
+        def empty_t(r):
             ht = ht_pool.tile([P, GROUPS, RT, P], BF16, name="ht", tag="ht")
-            nc.scalar.copy(out=ht[:], in_=tp[:])
+            nc.scalar.copy(out=ht[:], in_=tps[r][:])
             hts[r] = ht
 
         def new_grp(r):
@@ -198,36 +206,44 @@ def tile_switchnet_fstar_pb_t_kernel(tc, h_switch, k2, b2, k3, b3, out):
             nc.vector.tensor_tensor(
                 out=ysbs[r][:, a, i * HALF:(i + 1) * HALF], in0=yps[(r, k)][:],
                 in1=b3f[:, i * HALF:(i + 1) * HALF], op=ADD)
-            if r == ROUNDS - 1 and i == 1:
-                t = RT * r + a
+            t = RT * r + a
+            if r == ROUNDS - 1 and k == 1:
                 nc.sync.dma_start(out=out_view[:, t:t + 1, :], in_=ysbs[r][:, a:a + 1, :])
+            if r == ROUNDS - 1 and k >= 2:
+                nc.sync.dma_start(
+                    out=out_view[:, t:t + 1, i * HALF:(i + 1) * HALF],
+                    in_=ysbs[r][:, a:a + 1, i * HALF:(i + 1) * HALF])
             if r < ROUNDS - 1 and k == 3:
                 nc.sync.dma_start(out=out_view[:, RT * r:RT * (r + 1), :], in_=ysbs[r][:])
 
         transposes(0)
+        empty_t(0)
         spread_biases()
         regroup_k3(nc.vector.tensor_copy, 0, 0, HALF)
         stage1_on_vector(0)
+        regroup_k3(nc.vector.tensor_copy, 1, 0, HALF)
         transposes(1)
-        regroup_k3(nc.scalar.copy, 1, HALF // 2, HALF)
-        regroup_k3(nc.vector.tensor_copy, 1, 0, HALF // 2)
+        empty_t(1)
+        transposes(2)
+        empty_t(2)
         stage1(1)
         add_b2(1, 0)
-        transposes(2)
         add_b2(1, 1)
         transposes(3)
+        empty_t(3)
         quantise_k3(0)
         quantise_k3(1)
         quantise(0)
         regroup(1)
+        for k in range(4):
+            mx_pass(0, k)
         stage1(2)
         add_b2(2, 0)
         add_b2(2, 1)
-        for k in range(4):
-            mx_pass(0, k)
         for s in range(ROUNDS):
             if s + 4 < ROUNDS:
                 transposes(s + 4)
+                empty_t(s + 4)
             if s + 3 < ROUNDS:
                 stage1(s + 3)
                 add_b2(s + 3, 0)

@@ -48,6 +48,10 @@ def tile_switchnet_fstar_pb_t_kernel(tc, h_switch, k2, b2, k3, b3, out):
         b3z = const.tile([P, L], BF16, name="b3z")
         ones = const.tile([P, P], BF16, name="ones")
         ident = const.tile([P, P], BF16, name="ident")
+        b2s = const.tile([GROUPS, P], BF16, name="b2s")
+        b3s = const.tile([1, L], BF16, name="b3s")
+        nc.sync.dma_start(out=b2s[:], in_=b2.rearrange("o j r -> (o j) r"))
+        nc.sync.dma_start(out=b3s[:], in_=b3.rearrange("o j l -> (o j) l"))
         nc.vector.memset(b2z[:], 0.0)
         nc.vector.memset(b3z[:], 0.0)
         nc.vector.memset(ones[:], 1.0)
@@ -76,27 +80,31 @@ def tile_switchnet_fstar_pb_t_kernel(tc, h_switch, k2, b2, k3, b3, out):
             hc, start, n = h_tiles[c]
             nc.sync.dma_start(out=hc[:], in_=h_view[:, start:start + n, :])
 
-        load_h(0)
-        nc.sync.dma_start(out=k2_sb[:], in_=k2.rearrange("j k m -> k j m"))
-        nc.sync.dma_start(out=b2z[0:GROUPS, :], in_=b2.rearrange("o j r -> (o j) r"))
-        nc.sync.dma_start(out=b3z[0:1, :], in_=b3.rearrange("o j l -> (o j) l"))
-        load_h(1)
-        for i in range(2):
+        def load_k3(i):
             nc.sync.dma_start(out=k3r[i][:], in_=k3_view[:, :, i * HALF:(i + 1) * HALF])
+
+        load_h(0)
+        load_k3(0)
+        nc.sync.dma_start(out=k2_sb[:], in_=k2.rearrange("j k m -> k j m"))
+        load_h(1)
+        load_k3(1)
         for c in range(2, len(H_CHUNKS)):
             load_h(c)
+        nc.vector.tensor_copy(out=b2z[0:GROUPS, :], in_=b2s[:])
+        nc.vector.tensor_copy(out=b3z[0:1, :], in_=b3s[:])
 
         b2f = const.tile([P, GROUPS], F32, name="b2f")
         b3f = const.tile([P, L], F32, name="b3f")
 
-        def spread_biases():
+        def spread_b2():
             tpb = ps_t.tile([P, GROUPS, RT, P], BF16, name="tp", tag="tp")
             nc.tensor.transpose(tpb[:, 0, 0, :], b2z[:], ident[:])
             nc.vector.tensor_copy(out=b2f[:], in_=tpb[:, 0, 0, 0:GROUPS])
-            for i in range(2):
-                yb = ps_y.tile([P, HALF], F32, name="y", tag="y")
-                nc.tensor.matmul(yb[:], lhsT=ones[:], rhs=b3z[:, i * HALF:(i + 1) * HALF], start=True, stop=True)
-                nc.scalar.copy(out=b3f[:, i * HALF:(i + 1) * HALF], in_=yb[:])
+
+        def spread_b3(i):
+            yb = ps_y.tile([P, HALF], F32, name="y", tag="y")
+            nc.tensor.matmul(yb[:], lhsT=ones[:], rhs=b3z[:, i * HALF:(i + 1) * HALF], start=True, stop=True)
+            nc.scalar.copy(out=b3f[:, i * HALF:(i + 1) * HALF], in_=yb[:])
 
         def regroup_k3(engine_copy, i, n0, n1):
             engine_copy(
@@ -136,18 +144,19 @@ def tile_switchnet_fstar_pb_t_kernel(tc, h_switch, k2, b2, k3, b3, out):
         def new_grp(r):
             grps[r] = grp_pool.tile([P, RB, GROUPS], BF16, name="grp", tag="grp", align_bytes=64)
 
-        def stage1_on_vector(r):
-            new_grp(r)
-            for a in range(RT):
-                g = ps_g.tile([P, GROUPS, P], F32, name="g", tag="g")
-                for j in range(GROUPS):
-                    nc.tensor.matmul(g[:, j, :], lhsT=k2_sb[:, j, :], rhs=hts[r][:, j, a, :], start=True, stop=True)
-                nc.vector.tensor_tensor(
-                    out=grps[r][:, a * P:(a + 1) * P, :],
-                    in0=g[:].rearrange("p j b -> p b j"),
-                    in1=b2f[:].unsqueeze(1).to_broadcast([P, P, GROUPS]),
-                    op=ADD,
-                )
+        def stage1_tile(r, a):
+            g = ps_g.tile([P, GROUPS, P], F32, name="g", tag="g")
+            for j in range(GROUPS):
+                nc.tensor.matmul(g[:, j, :], lhsT=k2_sb[:, j, :], rhs=hts[r][:, j, a, :], start=True, stop=True)
+            gps[(r, a)] = g
+
+        def add_b2_on_vector(r, a):
+            nc.vector.tensor_tensor(
+                out=grps[r][:, a * P:(a + 1) * P, :],
+                in0=gps[(r, a)][:].rearrange("p j b -> p b j"),
+                in1=b2f[:].unsqueeze(1).to_broadcast([P, P, GROUPS]),
+                op=ADD,
+            )
 
         def stage1(r):
             gps[r] = []
@@ -216,50 +225,57 @@ def tile_switchnet_fstar_pb_t_kernel(tc, h_switch, k2, b2, k3, b3, out):
             if r < ROUNDS - 1 and k == 3:
                 nc.sync.dma_start(out=out_view[:, RT * r:RT * (r + 1), :], in_=ysbs[r][:])
 
+        spread_b2()
         transposes(0)
         empty_t(0)
-        spread_biases()
+        spread_b3(0)
+        stage1_tile(0, 0)
+        stage1_tile(0, 1)
+        spread_b3(1)
+        new_grp(0)
         regroup_k3(nc.vector.tensor_copy, 0, 0, HALF)
-        stage1_on_vector(0)
+        add_b2_on_vector(0, 0)
+        quantise_k3(0)
+        add_b2_on_vector(0, 1)
         regroup_k3(nc.vector.tensor_copy, 1, 0, HALF)
+        quantise(0)
+        quantise_k3(1)
         transposes(1)
         empty_t(1)
-        transposes(2)
-        empty_t(2)
         stage1(1)
         add_b2(1, 0)
         add_b2(1, 1)
-        transposes(3)
-        empty_t(3)
-        quantise_k3(0)
-        quantise_k3(1)
-        quantise(0)
         regroup(1)
-        for k in range(4):
-            mx_pass(0, k)
-        stage1(2)
-        add_b2(2, 0)
-        add_b2(2, 1)
-        for s in range(ROUNDS):
+        transposes(2)
+        empty_t(2)
+        for s in range(-1, ROUNDS):
+            late = s <= 0
             if s + 4 < ROUNDS:
                 transposes(s + 4)
                 empty_t(s + 4)
-            if s + 3 < ROUNDS:
+            if s + 3 < ROUNDS and not late:
                 stage1(s + 3)
                 add_b2(s + 3, 0)
                 add_b2(s + 3, 1)
-            empty_y(s, 0)
-            empty_y(s, 1)
-            if s + 1 < ROUNDS:
-                quantise(s + 1)
-            if s + 2 < ROUNDS:
-                regroup(s + 2)
+            if s >= 0:
+                empty_y(s, 0)
+                empty_y(s, 1)
+                if s + 1 < ROUNDS:
+                    quantise(s + 1)
+                if s + 2 < ROUNDS:
+                    regroup(s + 2)
             if s + 1 < ROUNDS:
                 mx_pass(s + 1, 0)
                 mx_pass(s + 1, 1)
-            empty_y(s, 2)
+            if late:
+                stage1(s + 3)
+                add_b2(s + 3, 0)
+                add_b2(s + 3, 1)
+            if s >= 0:
+                empty_y(s, 2)
             if s + 1 < ROUNDS:
                 mx_pass(s + 1, 2)
-            empty_y(s, 3)
+            if s >= 0:
+                empty_y(s, 3)
             if s + 1 < ROUNDS:
                 mx_pass(s + 1, 3)

from contextlib import ExitStack

import concourse.masks as masks
import concourse.mybir as mybir

BF16 = mybir.dt.bfloat16
F32 = mybir.dt.float32
U32 = mybir.dt.uint32
U8 = mybir.dt.uint8
FP8X4 = mybir.dt.float8_e4m3fn_x4
ADD = mybir.AluOpType.add
MULT = mybir.AluOpType.mult
IDENT = mybir.ActivationFunctionType.Identity

P = 128
GROUPS = 4
SAMPLES = 4096
TILES = SAMPLES // P
RT = 2
RB = RT * P
ROUNDS = TILES // RT
L = 1024
HALF = 512
H_CHUNKS = [2, 2, 4, 8, 8, 8]

FLOPS = 2 * SAMPLES * GROUPS * P * P + 2 * SAMPLES * GROUPS * P * L


def tile_switchnet_fstar_pb_t_kernel(tc, h_switch, k2, b2, k3, b3, out):
    nc = tc.nc
    h_view = h_switch.rearrange("(p t) j r -> p t (j r)", t=TILES)
    out_view = out.rearrange("(p t) x y c -> p t (x y c)", t=TILES)
    k3_view = k3.rearrange("o (t p) n -> p (o t) n", p=P)

    with ExitStack() as ctx:
        ctx.enter_context(tc.manual_schedule())
        const = ctx.enter_context(tc.tile_pool(name="const", bufs=1))
        ht_pool = ctx.enter_context(tc.tile_pool(name="ht", bufs=4))
        gs_pool = ctx.enter_context(tc.tile_pool(name="gs", bufs=3))
        grp_pool = ctx.enter_context(tc.tile_pool(name="grp", bufs=1))
        q_pool = ctx.enter_context(tc.tile_pool(name="q", bufs=3))
        y_pool = ctx.enter_context(tc.tile_pool(name="ysb", bufs=5))
        ps_t = ctx.enter_context(tc.psum_pool(name="pst", bufs=2))
        ps_g = ctx.enter_context(tc.psum_pool(name="psg", bufs=2))
        ps_y = ctx.enter_context(tc.psum_pool(name="psy", bufs=4))

        b2z = const.tile([P, P], BF16, name="b2z")
        b3z = const.tile([P, L], BF16, name="b3z")
        ones = const.tile([P, P], BF16, name="ones")
        ident = const.tile([P, P], BF16, name="ident")
        b2s = const.tile([GROUPS, P], BF16, name="b2s")
        b3s = const.tile([1, L], BF16, name="b3s")
        nc.sync.dma_start(out=b2s[:], in_=b2.rearrange("o j r -> (o j) r"))
        nc.sync.dma_start(out=b3s[:], in_=b3.rearrange("o j l -> (o j) l"))
        nc.vector.memset(b2z[:], 0.0)
        nc.vector.memset(b3z[:], 0.0)
        nc.vector.memset(ones[:], 1.0)
        masks.make_identity(nc, ident[:])

        warm = const.tile([P, 2], F32, name="warm")
        nc.vector.memset(warm[:], 0.0)
        nc.scalar.activation(out=warm[:, 1:2], in_=warm[:, 0:1], func=IDENT, bias=0.0, scale=1.0)

        h_of = []
        h_tiles = []
        t0 = 0
        for c, n in enumerate(H_CHUNKS):
            hc = const.tile([P, n, GROUPS * P], BF16, name="h%d" % c)
            h_tiles.append((hc, t0, n))
            for i in range(n):
                h_of.append((hc, i))
            t0 += n
        k2_sb = const.tile([P, GROUPS, P], BF16, name="k2sb")
        k3r = [const.tile([P, GROUPS, HALF], BF16, name="k3r%d" % i) for i in range(2)]
        k3g = [const.tile([P, HALF, GROUPS], BF16, name="k3g%d" % i, align_bytes=64) for i in range(2)]
        k3c = const.tile([P, L], U32, name="k3c", align_bytes=64)
        k3s = const.tile([P, L], U8, name="k3s", align_bytes=64)

        def load_h(c):
            hc, start, n = h_tiles[c]
            nc.sync.dma_start(out=hc[:], in_=h_view[:, start:start + n, :])

        def load_k3(i):
            nc.sync.dma_start(out=k3r[i][:], in_=k3_view[:, :, i * HALF:(i + 1) * HALF])

        load_h(0)
        load_k3(0)
        nc.sync.dma_start(out=k2_sb[:], in_=k2.rearrange("j k m -> k j m"))
        load_h(1)
        load_k3(1)
        for c in range(2, len(H_CHUNKS)):
            load_h(c)
        nc.vector.tensor_copy(out=b2z[0:GROUPS, :], in_=b2s[:])
        nc.vector.tensor_copy(out=b3z[0:1, :], in_=b3s[:])

        b2f = const.tile([P, GROUPS], F32, name="b2f")
        b3f = const.tile([P, L], F32, name="b3f")

        def spread_b2():
            tpb = ps_t.tile([P, GROUPS, RT, P], BF16, name="tp", tag="tp")
            nc.tensor.transpose(tpb[:, 0, 0, :], b2z[:], ident[:])
            nc.vector.tensor_copy(out=b2f[:], in_=tpb[:, 0, 0, 0:GROUPS])

        def spread_b3(i):
            yb = ps_y.tile([P, HALF], F32, name="y", tag="y")
            nc.tensor.matmul(yb[:], lhsT=ones[:], rhs=b3z[:, i * HALF:(i + 1) * HALF], start=True, stop=True)
            nc.scalar.copy(out=b3f[:, i * HALF:(i + 1) * HALF], in_=yb[:])

        def regroup_k3(engine_copy, i, n0, n1):
            engine_copy(
                out=k3g[i][:, n0:n1, :].rearrange("p (c i) t -> p c t i", i=4),
                in_=k3r[i][:, :, n0:n1].rearrange("p t (c i) -> p c t i", i=4),
            )

        def quantise_k3(i):
            nc.vector.quantize_mx(
                out=k3c[:, i * HALF:(i + 1) * HALF].bitcast(FP8X4),
                scales=k3s[:, i * HALF:(i + 1) * HALF],
                in_=k3g[i][:].rearrange("p n t -> p (n t)"),
            )

        tps = {}
        hts = {}
        gps = {}
        gss = {}
        grps = {}
        qs = {}
        yps = {}
        ysbs = {}

        def transposes(r):
            tp = ps_t.tile([P, GROUPS, RT, P], BF16, name="tp", tag="tp")
            for a in range(RT):
                hc, off = h_of[RT * r + a]
                for j in range(GROUPS):
                    nc.tensor.transpose(tp[:, j, a, :], hc[:, off, j * P:(j + 1) * P], ident[:])
            tps[r] = tp

        def empty_t(r):
            ht = ht_pool.tile([P, GROUPS, RT, P], BF16, name="ht", tag="ht")
            nc.scalar.copy(out=ht[:], in_=tps[r][:])
            hts[r] = ht

        def new_grp(r):
            grps[r] = grp_pool.tile([P, RB, GROUPS], BF16, name="grp", tag="grp", align_bytes=64)

        def stage1_tile(r, a):
            g = ps_g.tile([P, GROUPS, P], F32, name="g", tag="g")
            for j in range(GROUPS):
                nc.tensor.matmul(g[:, j, :], lhsT=k2_sb[:, j, :], rhs=hts[r][:, j, a, :], start=True, stop=True)
            gps[(r, a)] = g

        def add_b2_on_vector(r, a):
            nc.vector.tensor_tensor(
                out=grps[r][:, a * P:(a + 1) * P, :],
                in0=gps[(r, a)][:].rearrange("p j b -> p b j"),
                in1=b2f[:].unsqueeze(1).to_broadcast([P, P, GROUPS]),
                op=ADD,
            )

        def stage1(r):
            gps[r] = []
            for hb in range(2):
                g = ps_g.tile([P, 2, RB], F32, name="g", tag="g")
                for jj in range(2):
                    j = 2 * hb + jj
                    nc.tensor.matmul(
                        g[:, jj, :], lhsT=k2_sb[:, j, :],
                        rhs=hts[r][:, j, :, :].rearrange("p a b -> p (a b)"), start=True, stop=True)
                gps[r].append(g)
            gss[r] = gs_pool.tile([P, GROUPS, RB], BF16, name="gs", tag="gs")

        def add_b2(r, hb):
            for jj in range(2):
                j = 2 * hb + jj
                nc.scalar.activation(
                    out=gss[r][:, j, :], in_=gps[r][hb][:, jj, :], func=IDENT,
                    bias=b2f[:, j:j + 1], scale=1.0)

        def regroup(r):
            new_grp(r)
            nc.gpsimd.tensor_scalar(
                out=grps[r][:], in0=gss[r][:].rearrange("p j b -> p b j"),
                scalar1=1.0, scalar2=0.0, op0=MULT, op1=ADD)

        def quantise(r):
            codes = q_pool.tile([P, RB], U32, name="codes", tag="codes", align_bytes=64)
            scl = q_pool.tile([P, RB], U8, name="scl", tag="scl", align_bytes=64)
            nc.vector.quantize_mx(
                out=codes[:].bitcast(FP8X4),
                scales=scl[:],
                in_=grps[r][:].rearrange("p b j -> p (b j)"),
            )
            qs[r] = (codes, scl)

        def mx_pass(r, k):
            a, i = k // 2, k % 2
            codes, scl = qs[r]
            y = ps_y.tile([P, HALF], F32, name="y", tag="y")
            nc.tensor.matmul_mx(
                out=y[:],
                lhsT=codes[:, a * P:(a + 1) * P].bitcast(FP8X4),
                lhsT_scale=scl[:, a * P:(a + 1) * P],
                rhs=k3c[:, i * HALF:(i + 1) * HALF].bitcast(FP8X4),
                rhs_scale=k3s[:, i * HALF:(i + 1) * HALF],
                start=True,
                stop=True,
            )
            yps[(r, k)] = y

        def empty_y(r, k):
            a, i = k // 2, k % 2
            if k == 0:
                ysbs[r] = y_pool.tile([P, RT, L], F32, name="ysb", tag="ysb")
            nc.vector.tensor_tensor(
                out=ysbs[r][:, a, i * HALF:(i + 1) * HALF], in0=yps[(r, k)][:],
                in1=b3f[:, i * HALF:(i + 1) * HALF], op=ADD)
            t = RT * r + a
            if r == ROUNDS - 1 and k == 1:
                nc.sync.dma_start(out=out_view[:, t:t + 1, :], in_=ysbs[r][:, a:a + 1, :])
            if r == ROUNDS - 1 and k >= 2:
                nc.sync.dma_start(
                    out=out_view[:, t:t + 1, i * HALF:(i + 1) * HALF],
                    in_=ysbs[r][:, a:a + 1, i * HALF:(i + 1) * HALF])
            if r < ROUNDS - 1 and k == 3:
                nc.sync.dma_start(out=out_view[:, RT * r:RT * (r + 1), :], in_=ysbs[r][:])

        spread_b2()
        transposes(0)
        empty_t(0)
        spread_b3(0)
        stage1_tile(0, 0)
        stage1_tile(0, 1)
        spread_b3(1)
        new_grp(0)
        regroup_k3(nc.vector.tensor_copy, 0, 0, HALF)
        add_b2_on_vector(0, 0)
        quantise_k3(0)
        add_b2_on_vector(0, 1)
        regroup_k3(nc.vector.tensor_copy, 1, 0, HALF)
        quantise(0)
        quantise_k3(1)
        transposes(1)
        empty_t(1)
        stage1(1)
        add_b2(1, 0)
        add_b2(1, 1)
        regroup(1)
        transposes(2)
        empty_t(2)
        for s in range(-1, ROUNDS):
            late = s <= 0
            if s + 4 < ROUNDS:
                transposes(s + 4)
                empty_t(s + 4)
            if s + 3 < ROUNDS and not late:
                stage1(s + 3)
                add_b2(s + 3, 0)
                add_b2(s + 3, 1)
            if s >= 0:
                empty_y(s, 0)
                empty_y(s, 1)
                if s + 1 < ROUNDS:
                    quantise(s + 1)
                if s + 2 < ROUNDS:
                    regroup(s + 2)
            if s + 1 < ROUNDS:
                mx_pass(s + 1, 0)
                mx_pass(s + 1, 1)
            if late:
                stage1(s + 3)
                add_b2(s + 3, 0)
                add_b2(s + 3, 1)
            if s >= 0:
                empty_y(s, 2)
            if s + 1 < ROUNDS:
                mx_pass(s + 1, 2)
            if s >= 0:
                empty_y(s, 3)
            if s + 1 < ROUNDS:
                mx_pass(s + 1, 3)
